import numpy as np
import ml_dtypes


def mxq(x, axis, fmt="e4m3"):
    dtype, down = {"e4m3": (ml_dtypes.float8_e4m3fn, 7), "e5m2": (ml_dtypes.float8_e5m2, 14)}[fmt]
    v = np.moveaxis(np.asarray(x, np.float32).astype(ml_dtypes.bfloat16).astype(np.float64), axis, -1)
    blocks = v.reshape(v.shape[:-1] + (-1, 32))
    amax = np.abs(blocks).max(-1, keepdims=True)
    byte = np.maximum(np.where(amax > 0, np.frexp(amax)[1] - 1 + 127, 0) - down, 1)
    scale = np.exp2(byte - 127.0)
    codes = (blocks / scale).astype(np.float32).astype(dtype).astype(np.float64)
    return np.moveaxis((codes * scale).reshape(v.shape), -1, axis)


WIDE = False


def mx_kscale(k):
    if not WIDE:
        return np.ones(k)
    levels = np.array([10, -10, 5, -5, 0])
    if k % 512:
        return np.exp2(np.random.permutation(np.resize(levels, k // 32))).repeat(32)
    a = np.empty((k // 512, 16))
    for p in range(k // 512):
        a[p, :8] = np.random.permutation(np.resize(levels, 8))
        for g in range(8):
            far = levels[np.abs(levels - a[p, g]) >= 10]
            a[p, g + 8] = far[np.random.randint(len(far))]
    return np.exp2(a.ravel()).repeat(32)


BF16 = ml_dtypes.bfloat16


def bf(x):
    return np.asarray(x, np.float32).astype(BF16)


def f64(x):
    return np.asarray(x).astype(np.float64)


B, T, D, LAT, H = 2, 2048, 512, 1024, 4
L = LAT // H
SQ = 2.0


def setup_inputs():
    s = mx_kscale(D)
    return {"query": bf(np.random.standard_normal((B, T, D)) * s),
            "wq": bf(np.random.standard_normal((D, LAT)) * SQ / np.sqrt(D) / s[:, None])}


def reference(query, wq):
    Q = mxq(f64(query), 2, "e4m3") @ mxq(f64(wq), 0, "e4m3")
    Q = Q.transpose(1, 0, 2).reshape(T, B, H, L)
    e = np.exp(Q - Q.max(-1, keepdims=True))
    return e / e.sum(-1, keepdims=True)

@@ -1,0 +1,214 @@
+from contextlib import ExitStack
+
+import concourse.mybir as mybir
+from concourse.masks import make_identity
+
+F32 = mybir.dt.float32
+BF16 = mybir.dt.bfloat16
+U32 = mybir.dt.uint32
+U8 = mybir.dt.uint8
+FP8X4 = mybir.dt.float8_e4m3fn_x4
+ALU = mybir.AluOpType
+ACT = mybir.ActivationFunctionType
+
+P = 128
+BATCH = 2
+TOKENS = 2048
+DEPTH = 512
+SLOTS = 1024
+HEADS = 4
+HEAD = SLOTS // HEADS
+BANK = 512
+HALVES = SLOTS // BANK
+ROUNDS = TOKENS // P
+TILES = ROUNDS * BATCH
+WORDS = DEPTH // 2
+GPSIMD_HEADS_EARLY = 3
+GPSIMD_HEADS_LATE = 2
+AHEAD = 4
+
+FLOPS = 2 * BATCH * TOKENS * DEPTH * SLOTS
+
+
+def tile_latentattention_pb_t_kernel(tc, query, wq, out):
+    nc = tc.nc
+    with ExitStack() as ctx:
+        keep = ctx.enter_context(tc.tile_pool(name="keep", bufs=1))
+        small = ctx.enter_context(tc.tile_pool(name="small", bufs=8))
+        results = ctx.enter_context(tc.tile_pool(name="results", bufs=8))
+        psum_t = ctx.enter_context(tc.psum_pool(name="psum_t", bufs=2))
+        psum_q = ctx.enter_context(tc.psum_pool(name="psum_q", bufs=6))
+
+        query_view = query.rearrange("b (p j) d -> p b j d", j=ROUNDS)
+        out_view = out.rearrange("(p j) b h l -> p j b (h l)", j=ROUNDS)
+        wq_view = wq.rearrange("(q t) c -> q t c", t=4)
+
+        q_words = {}
+
+        def load_queries(first, count):
+            piece = keep.tile([P, BATCH, count, DEPTH], BF16, name="q_raw%d" % first)
+            nc.sync.dma_start(out=piece[:], in_=query_view[:, :, first : first + count, :])
+            for j in range(count):
+                q_words[first + j] = piece[:].bitcast(F32)[:, :, j, :]
+
+        w_raw = [keep.tile([P, 4, BANK], BF16, name="w_raw%d" % half) for half in range(HALVES)]
+        load_queries(0, 1)
+        for half in range(HALVES):
+            nc.sync.dma_start(out=w_raw[half][:], in_=wq_view[:, :, half * BANK : (half + 1) * BANK])
+        loaded = 1
+        for doubling in range(4):
+            load_queries(loaded, loaded)
+            loaded = 2 * loaded
+        assert loaded == ROUNDS
+
+        ident = keep.tile([P, P], F32)
+        make_identity(nc, ident[:])
+        zero = keep.tile([P, 1], F32)
+        one = keep.tile([P, 1], F32)
+        nc.vector.memset(zero[:], 0.0)
+        nc.scalar.activation(out=one[:], in_=zero[:], func=ACT.Exp)
+
+        q_grouped = keep.tile([P, ROUNDS, BATCH, P, 4], BF16, align_bytes=64)
+        q_codes = keep.tile([P, ROUNDS, BATCH * P], U32, align_bytes=64)
+        q_scales = keep.tile([P, ROUNDS, BATCH * P], U8, align_bytes=64)
+        w_grouped = keep.tile([P, SLOTS, 4], BF16, align_bytes=64)
+        w_codes = keep.tile([P, SLOTS], U32, align_bytes=64)
+        w_scales = keep.tile([P, SLOTS], U8, align_bytes=64)
+
+        turned = {}
+
+        def transpose_queries(j):
+            turned[j] = psum_t.tile([P, BATCH, 2, P], F32, name="turned")
+            for b in range(BATCH):
+                for u in range(2):
+                    nc.tensor.transpose(
+                        turned[j][:, b, u, :], q_words[j][:, b, u : WORDS : 2], ident[:]
+                    )
+
+        def group_queries(j):
+            side_by_side = turned[j][:].rearrange("p b u r -> p b r u")
+            if j < AHEAD:
+                nc.scalar.copy(out=q_grouped[:, j].bitcast(F32), in_=side_by_side)
+            else:
+                nc.vector.tensor_copy(out=q_grouped[:, j].bitcast(F32), in_=side_by_side)
+
+        def quantise_queries(j):
+            nc.vector.quantize_mx(
+                out=q_codes[:, j, :].bitcast(FP8X4),
+                scales=q_scales[:, j, :],
+                in_=q_grouped[:, j].rearrange("p b r t -> p (b r t)"),
+            )
+
+        def group_weights(half):
+            cols = slice(half * BANK, (half + 1) * BANK)
+            nc.vector.tensor_copy(
+                out=w_grouped[:, cols, :].rearrange("p (c i) t -> p c t i", i=4),
+                in_=w_raw[half][:].rearrange("p t (c i) -> p c t i", i=4),
+            )
+
+        def quantise_weights(half):
+            cols = slice(half * BANK, (half + 1) * BANK)
+            nc.vector.quantize_mx(
+                out=w_codes[:, cols].bitcast(FP8X4),
+                scales=w_scales[:, cols],
+                in_=w_grouped[:, cols, :].rearrange("p c t -> p (c t)"),
+            )
+
+        scores = {}
+        neg_max = {}
+        sums = {}
+        weights = {}
+
+        def multiply(i):
+            j, b = divmod(i, BATCH)
+            for half in range(HALVES):
+                cols = slice(half * BANK, (half + 1) * BANK)
+                bank = psum_q.tile([P, BANK], F32, name="bank")
+                nc.tensor.matmul_mx(
+                    out=bank[:],
+                    lhsT=q_codes[:, j, b * P : (b + 1) * P].bitcast(FP8X4),
+                    lhsT_scale=q_scales[:, j, b * P : (b + 1) * P],
+                    rhs=w_codes[:, cols].bitcast(FP8X4),
+                    rhs_scale=w_scales[:, cols],
+                    start=True,
+                    stop=True,
+                )
+                scores[(i, half)] = bank
+
+        def maxima(i):
+            neg_max[i] = small.tile([P, HEADS], F32, name="neg_max")
+            for half in range(HALVES):
+                nc.vector.tensor_reduce(
+                    out=neg_max[i][:, 2 * half : 2 * half + 2],
+                    in_=scores[(i, half)][:].rearrange("p (h l) -> p h l", l=HEAD),
+                    axis=mybir.AxisListType.X,
+                    op=ALU.max,
+                    negate=True,
+                )
+
+        def exponentials(i):
+            weights[i] = results.tile([P, SLOTS], F32, name="weights")
+            sums[i] = small.tile([P, HEADS], F32, name="sums")
+            for h in range(HEADS):
+                half, side = divmod(h, 2)
+                nc.scalar.activation(
+                    out=weights[i][:, h * HEAD : (h + 1) * HEAD],
+                    in_=scores[(i, half)][:, side * HEAD : (side + 1) * HEAD],
+                    func=ACT.Exp,
+                    bias=neg_max[i][:, h : h + 1],
+                    scale=1.0,
+                    accum_out=sums[i][:, h : h + 1],
+                )
+
+        def normalise(i):
+            j, b = divmod(i, BATCH)
+            inverse = small.tile([P, HEADS], F32)
+            nc.vector.reciprocal(out=inverse[:], in_=sums[i][:])
+            gpsimd_heads = GPSIMD_HEADS_EARLY if j + AHEAD < ROUNDS else GPSIMD_HEADS_LATE
+            for h in range(HEADS):
+                head = weights[i][:, h * HEAD : (h + 1) * HEAD]
+                if h < gpsimd_heads:
+                    nc.gpsimd.tensor_scalar(
+                        out=head, in0=head, scalar1=inverse[:, h : h + 1], scalar2=0.0,
+                        op0=ALU.mult, op1=ALU.add,
+                    )
+                elif h < HEADS - 1:
+                    nc.vector.tensor_scalar(
+                        out=head, in0=head, scalar1=inverse[:, h : h + 1], scalar2=None,
+                        op0=ALU.mult,
+                    )
+                else:
+                    nc.scalar.activation(
+                        out=head, in_=head, func=ACT.Copy, scale=inverse[:, h : h + 1]
+                    )
+            nc.sync.dma_start(out=out_view[:, j, b, :], in_=weights[i][:])
+
+        with tc.manual_schedule():
+            transpose_queries(0)
+            group_queries(0)
+            quantise_queries(0)
+            for half in range(HALVES):
+                group_weights(half)
+            for half in range(HALVES):
+                quantise_weights(half)
+            for j in range(1, AHEAD):
+                transpose_queries(j)
+                group_queries(j)
+            quantise_queries(1)
+            multiply(0)
+            multiply(1)
+            for i in range(TILES):
+                j, b = divmod(i, BATCH)
+                if b == 0 and j + AHEAD < ROUNDS:
+                    transpose_queries(j + AHEAD)
+                if i + 2 < TILES:
+                    multiply(i + 2)
+                maxima(i)
+                exponentials(i)
+                if b == 0 and j + AHEAD < ROUNDS:
+                    group_queries(j + AHEAD)
+                if b == 1 and j + 2 < ROUNDS:
+                    quantise_queries(j + 2)
+                if i >= 1:
+                    normalise(i - 1)
+            normalise(TILES - 1)

@@ -23,9 +23,8 @@ HALVES = SLOTS // BANK
 ROUNDS = TOKENS // P
 TILES = ROUNDS * BATCH
 WORDS = DEPTH // 2
-GPSIMD_HEADS_EARLY = 3
-GPSIMD_HEADS_LATE = 2
-AHEAD = 4
+AHEAD = 3
+LAG = 1
 
 FLOPS = 2 * BATCH * TOKENS * DEPTH * SLOTS
 
@@ -87,7 +86,7 @@ def tile_latentattention_pb_t_kernel(tc, query, wq, out):
 
         def group_queries(j):
             side_by_side = turned[j][:].rearrange("p b u r -> p b r u")
-            if j < AHEAD:
+            if j < 3:
                 nc.scalar.copy(out=q_grouped[:, j].bitcast(F32), in_=side_by_side)
             else:
                 nc.vector.tensor_copy(out=q_grouped[:, j].bitcast(F32), in_=side_by_side)
@@ -99,15 +98,17 @@ def tile_latentattention_pb_t_kernel(tc, query, wq, out):
                 in_=q_grouped[:, j].rearrange("p b r t -> p (b r t)"),
             )
 
-        def group_weights(half):
-            cols = slice(half * BANK, (half + 1) * BANK)
-            nc.vector.tensor_copy(
-                out=w_grouped[:, cols, :].rearrange("p (c i) t -> p c t i", i=4),
-                in_=w_raw[half][:].rearrange("p t (c i) -> p c t i", i=4),
-            )
+        def group_weights(h):
+            half, side = divmod(h, 2)
+            grouped = w_grouped[:, h * HEAD : (h + 1) * HEAD, :].rearrange("p (c i) t -> p c t i", i=4)
+            raw = w_raw[half][:, :, side * HEAD : (side + 1) * HEAD].rearrange("p t (c i) -> p c t i", i=4)
+            if side == 0:
+                nc.vector.tensor_copy(out=grouped, in_=raw)
+            else:
+                nc.scalar.copy(out=grouped, in_=raw)
 
-        def quantise_weights(half):
-            cols = slice(half * BANK, (half + 1) * BANK)
+        def quantise_weights(h):
+            cols = slice(h * HEAD, (h + 1) * HEAD)
             nc.vector.quantize_mx(
                 out=w_codes[:, cols].bitcast(FP8X4),
                 scales=w_scales[:, cols],
@@ -119,9 +120,9 @@ def tile_latentattention_pb_t_kernel(tc, query, wq, out):
         sums = {}
         weights = {}
 
-        def multiply(i):
+        def multiply(i, halves=range(HALVES)):
             j, b = divmod(i, BATCH)
-            for half in range(HALVES):
+            for half in halves:
                 cols = slice(half * BANK, (half + 1) * BANK)
                 bank = psum_q.tile([P, BANK], F32, name="bank")
                 nc.tensor.matmul_mx(
@@ -135,9 +136,10 @@ def tile_latentattention_pb_t_kernel(tc, query, wq, out):
                 )
                 scores[(i, half)] = bank
 
-        def maxima(i):
-            neg_max[i] = small.tile([P, HEADS], F32, name="neg_max")
-            for half in range(HALVES):
+        def maxima(i, halves=range(HALVES)):
+            if i not in neg_max:
+                neg_max[i] = small.tile([P, HEADS], F32, name="neg_max")
+            for half in halves:
                 nc.vector.tensor_reduce(
                     out=neg_max[i][:, 2 * half : 2 * half + 2],
                     in_=scores[(i, half)][:].rearrange("p (h l) -> p h l", l=HEAD),
@@ -146,10 +148,11 @@ def tile_latentattention_pb_t_kernel(tc, query, wq, out):
                     negate=True,
                 )
 
-        def exponentials(i):
-            weights[i] = results.tile([P, SLOTS], F32, name="weights")
-            sums[i] = small.tile([P, HEADS], F32, name="sums")
-            for h in range(HEADS):
+        def exponentials(i, heads=range(HEADS)):
+            if i not in weights:
+                weights[i] = results.tile([P, SLOTS], F32, name="weights")
+                sums[i] = small.tile([P, HEADS], F32, name="sums")
+            for h in heads:
                 half, side = divmod(h, 2)
                 nc.scalar.activation(
                     out=weights[i][:, h * HEAD : (h + 1) * HEAD],
@@ -164,15 +167,15 @@ def tile_latentattention_pb_t_kernel(tc, query, wq, out):
             j, b = divmod(i, BATCH)
             inverse = small.tile([P, HEADS], F32)
             nc.vector.reciprocal(out=inverse[:], in_=sums[i][:])
-            gpsimd_heads = GPSIMD_HEADS_EARLY if j + AHEAD < ROUNDS else GPSIMD_HEADS_LATE
+            who = "GGGS" if j + 3 < ROUNDS else ("GGVS" if i < TILES - 2 else "GVVV")
             for h in range(HEADS):
                 head = weights[i][:, h * HEAD : (h + 1) * HEAD]
-                if h < gpsimd_heads:
+                if who[h] == "G":
                     nc.gpsimd.tensor_scalar(
                         out=head, in0=head, scalar1=inverse[:, h : h + 1], scalar2=0.0,
                         op0=ALU.mult, op1=ALU.add,
                     )
-                elif h < HEADS - 1:
+                elif who[h] == "V":
                     nc.vector.tensor_scalar(
                         out=head, in0=head, scalar1=inverse[:, h : h + 1], scalar2=None,
                         op0=ALU.mult,
@@ -186,29 +189,48 @@ def tile_latentattention_pb_t_kernel(tc, query, wq, out):
         with tc.manual_schedule():
             transpose_queries(0)
             group_queries(0)
+            group_weights(0)
+            group_weights(1)
             quantise_queries(0)
-            for half in range(HALVES):
-                group_weights(half)
-            for half in range(HALVES):
-                quantise_weights(half)
-            for j in range(1, AHEAD):
-                transpose_queries(j)
-                group_queries(j)
+            quantise_weights(0)
+            quantise_weights(1)
+            multiply(0, [0])
+            multiply(1, [0])
+            transpose_queries(1)
+            group_weights(2)
+            group_weights(3)
+            maxima(0, [0])
+            exponentials(0, [0, 1])
+            quantise_weights(2)
+            quantise_weights(3)
+            multiply(0, [1])
+            multiply(1, [1])
+            maxima(1, [0])
+            group_queries(1)
+            maxima(0, [1])
+            exponentials(0, [2, 3])
+            exponentials(1, [0, 1])
+            transpose_queries(2)
             quantise_queries(1)
-            multiply(0)
-            multiply(1)
-            for i in range(TILES):
+            multiply(2)
+            maxima(1, [1])
+            exponentials(1, [2, 3])
+            group_queries(2)
+            multiply(3)
+            normalise(0)
+            for i in range(2, TILES):
                 j, b = divmod(i, BATCH)
-                if b == 0 and j + AHEAD < ROUNDS:
-                    transpose_queries(j + AHEAD)
-                if i + 2 < TILES:
-                    multiply(i + 2)
+                if b == 0 and j + AHEAD - 1 < ROUNDS:
+                    transpose_queries(j + AHEAD - 1)
                 maxima(i)
                 exponentials(i)
-                if b == 0 and j + AHEAD < ROUNDS:
-                    group_queries(j + AHEAD)
-                if b == 1 and j + 2 < ROUNDS:
-                    quantise_queries(j + 2)
-                if i >= 1:
-                    normalise(i - 1)
-            normalise(TILES - 1)
+                if b == 0 and j + 1 < ROUNDS:
+                    quantise_queries(j + 1)
+                if i + 2 < TILES:
+                    multiply(i + 2)
+                if b == 1 and j + AHEAD - 1 < ROUNDS:
+                    group_queries(j + AHEAD - 1)
+                if i >= LAG:
+                    normalise(i - LAG)
+            for i in range(TILES - LAG, TILES):
+                normalise(i)

@@ -23,8 +23,6 @@ HALVES = SLOTS // BANK
 ROUNDS = TOKENS // P
 TILES = ROUNDS * BATCH
 WORDS = DEPTH // 2
-AHEAD = 3
-LAG = 1
 
 FLOPS = 2 * BATCH * TOKENS * DEPTH * SLOTS
 
@@ -33,8 +31,8 @@ def tile_latentattention_pb_t_kernel(tc, query, wq, out):
     nc = tc.nc
     with ExitStack() as ctx:
         keep = ctx.enter_context(tc.tile_pool(name="keep", bufs=1))
-        small = ctx.enter_context(tc.tile_pool(name="small", bufs=8))
-        results = ctx.enter_context(tc.tile_pool(name="results", bufs=8))
+        small = ctx.enter_context(tc.tile_pool(name="small", bufs=12))
+        results = ctx.enter_context(tc.tile_pool(name="results", bufs=12))
         psum_t = ctx.enter_context(tc.psum_pool(name="psum_t", bufs=2))
         psum_q = ctx.enter_context(tc.psum_pool(name="psum_q", bufs=6))
 
@@ -86,7 +84,7 @@ def tile_latentattention_pb_t_kernel(tc, query, wq, out):
 
         def group_queries(j):
             side_by_side = turned[j][:].rearrange("p b u r -> p b r u")
-            if j < 3:
+            if j < 3 or j % 4 == 0:
                 nc.scalar.copy(out=q_grouped[:, j].bitcast(F32), in_=side_by_side)
             else:
                 nc.vector.tensor_copy(out=q_grouped[:, j].bitcast(F32), in_=side_by_side)
@@ -163,28 +161,42 @@ def tile_latentattention_pb_t_kernel(tc, query, wq, out):
                     accum_out=sums[i][:, h : h + 1],
                 )
 
-        def normalise(i):
-            j, b = divmod(i, BATCH)
-            inverse = small.tile([P, HEADS], F32)
-            nc.vector.reciprocal(out=inverse[:], in_=sums[i][:])
-            who = "GGGS" if j + 3 < ROUNDS else ("GGVS" if i < TILES - 2 else "GVVV")
-            for h in range(HEADS):
+        inverse = {}
+
+        def invert(i, heads=slice(0, HEADS)):
+            if i not in inverse:
+                inverse[i] = small.tile([P, HEADS], F32, name="inverse")
+            nc.vector.reciprocal(out=inverse[i][:, heads], in_=sums[i][:, heads])
+
+        def normalise(i, engines, heads=range(HEADS)):
+            for h in heads:
                 head = weights[i][:, h * HEAD : (h + 1) * HEAD]
-                if who[h] == "G":
+                who = assign(i)[h]
+                if who not in engines:
+                    continue
+                if who in "Gg":
                     nc.gpsimd.tensor_scalar(
-                        out=head, in0=head, scalar1=inverse[:, h : h + 1], scalar2=0.0,
+                        out=head, in0=head, scalar1=inverse[i][:, h : h + 1], scalar2=0.0,
                         op0=ALU.mult, op1=ALU.add,
                     )
-                elif who[h] == "V":
+                elif who in "Vv":
                     nc.vector.tensor_scalar(
-                        out=head, in0=head, scalar1=inverse[:, h : h + 1], scalar2=None,
+                        out=head, in0=head, scalar1=inverse[i][:, h : h + 1], scalar2=None,
                         op0=ALU.mult,
                     )
                 else:
                     nc.scalar.activation(
-                        out=head, in_=head, func=ACT.Copy, scale=inverse[:, h : h + 1]
+                        out=head, in_=head, func=ACT.Copy, scale=inverse[i][:, h : h + 1]
                     )
-            nc.sync.dma_start(out=out_view[:, j, b, :], in_=weights[i][:])
+
+        def store(i, heads=slice(0, SLOTS)):
+            j, b = divmod(i, BATCH)
+            nc.sync.dma_start(out=out_view[:, j, b, heads], in_=weights[i][:, heads])
+
+        def assign(i):
+            if i < TILES - 4:
+                return "GGGS"
+            return "GGVS" if i < TILES - 1 else "VVSV"
 
         with tc.manual_schedule():
             transpose_queries(0)
@@ -217,20 +229,41 @@ def tile_latentattention_pb_t_kernel(tc, query, wq, out):
             exponentials(1, [2, 3])
             group_queries(2)
             multiply(3)
-            normalise(0)
-            for i in range(2, TILES):
+            invert(0)
+            normalise(0, "G")
+            for i in range(2, TILES - 1):
                 j, b = divmod(i, BATCH)
-                if b == 0 and j + AHEAD - 1 < ROUNDS:
-                    transpose_queries(j + AHEAD - 1)
                 maxima(i)
-                exponentials(i)
+                exponentials(i, [0, 1])
+                if b == 1 and j + 2 < ROUNDS:
+                    group_queries(j + 2)
+                exponentials(i, [2, 3])
                 if b == 0 and j + 1 < ROUNDS:
                     quantise_queries(j + 1)
+                invert(i - 1)
+                if i == 2:
+                    normalise(0, "S")
+                    store(0)
+                normalise(i - 1, "GVS")
+                store(i - 1)
+                if b == 0 and j + 2 < ROUNDS:
+                    transpose_queries(j + 2)
                 if i + 2 < TILES:
                     multiply(i + 2)
-                if b == 1 and j + AHEAD - 1 < ROUNDS:
-                    group_queries(j + AHEAD - 1)
-                if i >= LAG:
-                    normalise(i - LAG)
-            for i in range(TILES - LAG, TILES):
-                normalise(i)
+            last = TILES - 1
+            maxima(last, [0])
+            invert(last - 1)
+            normalise(last - 1, "G")
+            maxima(last, [1])
+            exponentials(last, [0, 1])
+            normalise(last - 1, "S")
+            exponentials(last, [2, 3])
+            invert(last, slice(0, 2))
+            normalise(last - 1, "V")
+            store(last - 1)
+            normalise(last, "V", [0, 1])
+            store(last, slice(0, BANK))
+            invert(last, slice(2, 4))
+            normalise(last, "S", [2, 3])
+            normalise(last, "V", [2, 3])
+            store(last, slice(BANK, SLOTS))

@@ -84,7 +84,7 @@ def tile_latentattention_pb_t_kernel(tc, query, wq, out):
 
         def group_queries(j):
             side_by_side = turned[j][:].rearrange("p b u r -> p b r u")
-            if j < 3 or j % 4 == 0:
+            if j < 3:
                 nc.scalar.copy(out=q_grouped[:, j].bitcast(F32), in_=side_by_side)
             else:
                 nc.vector.tensor_copy(out=q_grouped[:, j].bitcast(F32), in_=side_by_side)
@@ -200,34 +200,34 @@ def tile_latentattention_pb_t_kernel(tc, query, wq, out):
 
         with tc.manual_schedule():
             transpose_queries(0)
-            group_queries(0)
             group_weights(0)
-            group_weights(1)
+            group_queries(0)
             quantise_queries(0)
+            group_weights(1)
             quantise_weights(0)
+            group_weights(3)
             quantise_weights(1)
             multiply(0, [0])
-            multiply(1, [0])
-            transpose_queries(1)
             group_weights(2)
-            group_weights(3)
+            multiply(1, [0])
             maxima(0, [0])
             exponentials(0, [0, 1])
+            transpose_queries(1)
             quantise_weights(2)
+            group_queries(1)
             quantise_weights(3)
             multiply(0, [1])
-            multiply(1, [1])
             maxima(1, [0])
-            group_queries(1)
+            exponentials(1, [0, 1])
+            multiply(1, [1])
             maxima(0, [1])
             exponentials(0, [2, 3])
-            exponentials(1, [0, 1])
             transpose_queries(2)
             quantise_queries(1)
+            group_queries(2)
             multiply(2)
             maxima(1, [1])
             exponentials(1, [2, 3])
-            group_queries(2)
             multiply(3)
             invert(0)
             normalise(0, "G")
@@ -238,14 +238,14 @@ def tile_latentattention_pb_t_kernel(tc, query, wq, out):
                 if b == 1 and j + 2 < ROUNDS:
                     group_queries(j + 2)
                 exponentials(i, [2, 3])
-                if b == 0 and j + 1 < ROUNDS:
-                    quantise_queries(j + 1)
                 invert(i - 1)
                 if i == 2:
                     normalise(0, "S")
                     store(0)
                 normalise(i - 1, "GVS")
                 store(i - 1)
+                if b == 0 and j + 1 < ROUNDS:
+                    quantise_queries(j + 1)
                 if b == 0 and j + 2 < ROUNDS:
                     transpose_queries(j + 2)
                 if i + 2 < TILES:

@@ -23,6 +23,7 @@ HALVES = SLOTS // BANK
 ROUNDS = TOKENS // P
 TILES = ROUNDS * BATCH
 WORDS = DEPTH // 2
+W2_ON_VECTOR = 192
 
 FLOPS = 2 * BATCH * TOKENS * DEPTH * SLOTS
 
@@ -46,12 +47,19 @@ def tile_latentattention_pb_t_kernel(tc, query, wq, out):
             piece = keep.tile([P, BATCH, count, DEPTH], BF16, name="q_raw%d" % first)
             nc.sync.dma_start(out=piece[:], in_=query_view[:, :, first : first + count, :])
             for j in range(count):
-                q_words[first + j] = piece[:].bitcast(F32)[:, :, j, :]
+                for b in range(BATCH):
+                    q_words[(first + j, b)] = piece[:].bitcast(F32)[:, b, j, :]
+
+        def load_first(b):
+            piece = keep.tile([P, DEPTH], BF16, name="q_first%d" % b)
+            nc.sync.dma_start(out=piece[:], in_=query_view[:, b, 0, :])
+            q_words[(0, b)] = piece[:].bitcast(F32)
 
         w_raw = [keep.tile([P, 4, BANK], BF16, name="w_raw%d" % half) for half in range(HALVES)]
-        load_queries(0, 1)
-        for half in range(HALVES):
-            nc.sync.dma_start(out=w_raw[half][:], in_=wq_view[:, :, half * BANK : (half + 1) * BANK])
+        nc.sync.dma_start(out=w_raw[0][:], in_=wq_view[:, :, :BANK])
+        load_first(0)
+        load_first(1)
+        nc.sync.dma_start(out=w_raw[1][:], in_=wq_view[:, :, BANK:])
         loaded = 1
         for doubling in range(4):
             load_queries(loaded, loaded)
@@ -74,36 +82,33 @@ def tile_latentattention_pb_t_kernel(tc, query, wq, out):
 
         turned = {}
 
-        def transpose_queries(j):
+        def transpose_queries(j, rows=range(BATCH)):
             turned[j] = psum_t.tile([P, BATCH, 2, P], F32, name="turned")
-            for b in range(BATCH):
+            for b in rows:
                 for u in range(2):
                     nc.tensor.transpose(
-                        turned[j][:, b, u, :], q_words[j][:, b, u : WORDS : 2], ident[:]
+                        turned[j][:, b, u, :], q_words[(j, b)][:, u : WORDS : 2], ident[:]
                     )
 
-        def group_queries(j):
-            side_by_side = turned[j][:].rearrange("p b u r -> p b r u")
-            if j < 3:
-                nc.scalar.copy(out=q_grouped[:, j].bitcast(F32), in_=side_by_side)
-            else:
-                nc.vector.tensor_copy(out=q_grouped[:, j].bitcast(F32), in_=side_by_side)
-
-        def quantise_queries(j):
-            nc.vector.quantize_mx(
-                out=q_codes[:, j, :].bitcast(FP8X4),
-                scales=q_scales[:, j, :],
-                in_=q_grouped[:, j].rearrange("p b r t -> p (b r t)"),
+        def group_queries(copy, j, rows=slice(0, BATCH)):
+            copy(
+                out=q_grouped[:, j, rows].bitcast(F32),
+                in_=turned[j][:, rows].rearrange("p b u r -> p b r u"),
             )
 
-        def group_weights(h):
-            half, side = divmod(h, 2)
-            grouped = w_grouped[:, h * HEAD : (h + 1) * HEAD, :].rearrange("p (c i) t -> p c t i", i=4)
-            raw = w_raw[half][:, :, side * HEAD : (side + 1) * HEAD].rearrange("p t (c i) -> p c t i", i=4)
-            if side == 0:
-                nc.vector.tensor_copy(out=grouped, in_=raw)
-            else:
-                nc.scalar.copy(out=grouped, in_=raw)
+        def quantise_queries(j, first=0, count=BATCH):
+            cols = slice(first * P, (first + count) * P)
+            nc.vector.quantize_mx(
+                out=q_codes[:, j, cols].bitcast(FP8X4),
+                scales=q_scales[:, j, cols],
+                in_=q_grouped[:, j, first : first + count].rearrange("p b r t -> p (b r t)"),
+            )
+
+        def group_weights(copy, first, count=HEAD):
+            half, at = divmod(first, BANK)
+            grouped = w_grouped[:, first : first + count, :].rearrange("p (c i) t -> p c t i", i=4)
+            raw = w_raw[half][:, :, at : at + count].rearrange("p t (c i) -> p c t i", i=4)
+            copy(out=grouped, in_=raw)
 
         def quantise_weights(h):
             cols = slice(h * HEAD, (h + 1) * HEAD)
@@ -174,12 +179,12 @@ def tile_latentattention_pb_t_kernel(tc, query, wq, out):
                 who = assign(i)[h]
                 if who not in engines:
                     continue
-                if who in "Gg":
+                if who == "G":
                     nc.gpsimd.tensor_scalar(
                         out=head, in0=head, scalar1=inverse[i][:, h : h + 1], scalar2=0.0,
                         op0=ALU.mult, op1=ALU.add,
                     )
-                elif who in "Vv":
+                elif who == "V":
                     nc.vector.tensor_scalar(
                         out=head, in0=head, scalar1=inverse[i][:, h : h + 1], scalar2=None,
                         op0=ALU.mult,
@@ -199,22 +204,26 @@ def tile_latentattention_pb_t_kernel(tc, query, wq, out):
             return "GGVS" if i < TILES - 1 else "VVSV"
 
         with tc.manual_schedule():
-            transpose_queries(0)
-            group_weights(0)
-            group_queries(0)
-            quantise_queries(0)
-            group_weights(1)
+            transpose_queries(0, [0])
+            group_weights(nc.vector.tensor_copy, 0)
+            group_weights(nc.scalar.copy, HEAD)
             quantise_weights(0)
-            group_weights(3)
+            group_queries(nc.scalar.copy, 0, slice(0, 1))
+            transpose_queries(0, [1])
             quantise_weights(1)
+            group_queries(nc.scalar.copy, 0, slice(1, 2))
+            quantise_queries(0, 0, 1)
+            group_weights(nc.scalar.copy, 2 * HEAD + W2_ON_VECTOR, HEAD - W2_ON_VECTOR)
             multiply(0, [0])
-            group_weights(2)
+            group_weights(nc.vector.tensor_copy, 2 * HEAD, W2_ON_VECTOR)
+            group_weights(nc.scalar.copy, 3 * HEAD)
+            quantise_queries(0, 1, 1)
             multiply(1, [0])
             maxima(0, [0])
             exponentials(0, [0, 1])
             transpose_queries(1)
             quantise_weights(2)
-            group_queries(1)
+            group_queries(nc.scalar.copy, 1)
             quantise_weights(3)
             multiply(0, [1])
             maxima(1, [0])
@@ -224,7 +233,7 @@ def tile_latentattention_pb_t_kernel(tc, query, wq, out):
             exponentials(0, [2, 3])
             transpose_queries(2)
             quantise_queries(1)
-            group_queries(2)
+            group_queries(nc.scalar.copy, 2)
             multiply(2)
             maxima(1, [1])
             exponentials(1, [2, 3])
@@ -236,7 +245,7 @@ def tile_latentattention_pb_t_kernel(tc, query, wq, out):
                 maxima(i)
                 exponentials(i, [0, 1])
                 if b == 1 and j + 2 < ROUNDS:
-                    group_queries(j + 2)
+                    group_queries(nc.vector.tensor_copy, j + 2)
                 exponentials(i, [2, 3])
                 invert(i - 1)
                 if i == 2:

@@ -12,6 +12,7 @@ ALU = mybir.AluOpType
 ACT = mybir.ActivationFunctionType
 
 P = 128
+PACK = 4
 BATCH = 2
 TOKENS = 2048
 DEPTH = 512
@@ -22,8 +23,8 @@ BANK = 512
 HALVES = SLOTS // BANK
 ROUNDS = TOKENS // P
 TILES = ROUNDS * BATCH
-WORDS = DEPTH // 2
-W2_ON_VECTOR = 192
+PAIRS = DEPTH // 2
+ON_VECTOR = 192
 
 FLOPS = 2 * BATCH * TOKENS * DEPTH * SLOTS
 
@@ -39,32 +40,26 @@ def tile_latentattention_pb_t_kernel(tc, query, wq, out):
 
         query_view = query.rearrange("b (p j) d -> p b j d", j=ROUNDS)
         out_view = out.rearrange("(p j) b h l -> p j b (h l)", j=ROUNDS)
-        wq_view = wq.rearrange("(q t) c -> q t c", t=4)
+        wq_view = wq.rearrange("(q t) c -> q t c", t=PACK)
 
-        q_words = {}
+        q_pairs = {}
+        w_raw = [keep.tile([P, PACK, BANK], BF16, name="w_raw%d" % half) for half in range(HALVES)]
 
-        def load_queries(first, count):
-            piece = keep.tile([P, BATCH, count, DEPTH], BF16, name="q_raw%d" % first)
-            nc.sync.dma_start(out=piece[:], in_=query_view[:, :, first : first + count, :])
-            for j in range(count):
+        def load_weights(half):
+            nc.sync.dma_start(out=w_raw[half][:], in_=wq_view[:, :, half * BANK : (half + 1) * BANK])
+
+        load_weights(0)
+        for b in range(BATCH):
+            row = keep.tile([P, DEPTH], BF16, name="q_first%d" % b)
+            nc.sync.dma_start(out=row[:], in_=query_view[:, b, 0, :])
+            q_pairs[(0, b)] = row[:].bitcast(F32)
+        load_weights(1)
+        for first in (1, 2, 4, 8):
+            piece = keep.tile([P, BATCH, first, DEPTH], BF16, name="q_raw%d" % first)
+            nc.sync.dma_start(out=piece[:], in_=query_view[:, :, first : 2 * first, :])
+            for j in range(first):
                 for b in range(BATCH):
-                    q_words[(first + j, b)] = piece[:].bitcast(F32)[:, b, j, :]
-
-        def load_first(b):
-            piece = keep.tile([P, DEPTH], BF16, name="q_first%d" % b)
-            nc.sync.dma_start(out=piece[:], in_=query_view[:, b, 0, :])
-            q_words[(0, b)] = piece[:].bitcast(F32)
-
-        w_raw = [keep.tile([P, 4, BANK], BF16, name="w_raw%d" % half) for half in range(HALVES)]
-        nc.sync.dma_start(out=w_raw[0][:], in_=wq_view[:, :, :BANK])
-        load_first(0)
-        load_first(1)
-        nc.sync.dma_start(out=w_raw[1][:], in_=wq_view[:, :, BANK:])
-        loaded = 1
-        for doubling in range(4):
-            load_queries(loaded, loaded)
-            loaded = 2 * loaded
-        assert loaded == ROUNDS
+                    q_pairs[(first + j, b)] = piece[:].bitcast(F32)[:, b, j, :]
 
         ident = keep.tile([P, P], F32)
         make_identity(nc, ident[:])
@@ -73,10 +68,10 @@ def tile_latentattention_pb_t_kernel(tc, query, wq, out):
         nc.vector.memset(zero[:], 0.0)
         nc.scalar.activation(out=one[:], in_=zero[:], func=ACT.Exp)
 
-        q_grouped = keep.tile([P, ROUNDS, BATCH, P, 4], BF16, align_bytes=64)
+        q_grouped = keep.tile([P, ROUNDS, BATCH, P, PACK], BF16, align_bytes=64)
         q_codes = keep.tile([P, ROUNDS, BATCH * P], U32, align_bytes=64)
         q_scales = keep.tile([P, ROUNDS, BATCH * P], U8, align_bytes=64)
-        w_grouped = keep.tile([P, SLOTS, 4], BF16, align_bytes=64)
+        w_grouped = keep.tile([P, SLOTS, PACK], BF16, align_bytes=64)
         w_codes = keep.tile([P, SLOTS], U32, align_bytes=64)
         w_scales = keep.tile([P, SLOTS], U8, align_bytes=64)
 
@@ -87,7 +82,7 @@ def tile_latentattention_pb_t_kernel(tc, query, wq, out):
             for b in rows:
                 for u in range(2):
                     nc.tensor.transpose(
-                        turned[j][:, b, u, :], q_words[(j, b)][:, u : WORDS : 2], ident[:]
+                        turned[j][:, b, u, :], q_pairs[(j, b)][:, u:PAIRS:2], ident[:]
                     )
 
         def group_queries(copy, j, rows=slice(0, BATCH)):
@@ -106,9 +101,10 @@ def tile_latentattention_pb_t_kernel(tc, query, wq, out):
 
         def group_weights(copy, first, count=HEAD):
             half, at = divmod(first, BANK)
-            grouped = w_grouped[:, first : first + count, :].rearrange("p (c i) t -> p c t i", i=4)
-            raw = w_raw[half][:, :, at : at + count].rearrange("p t (c i) -> p c t i", i=4)
-            copy(out=grouped, in_=raw)
+            copy(
+                out=w_grouped[:, first : first + count, :].rearrange("p (c i) t -> p c t i", i=4),
+                in_=w_raw[half][:, :, at : at + count].rearrange("p t (c i) -> p c t i", i=4),
+            )
 
         def quantise_weights(h):
             cols = slice(h * HEAD, (h + 1) * HEAD)
@@ -120,8 +116,8 @@ def tile_latentattention_pb_t_kernel(tc, query, wq, out):
 
         scores = {}
         neg_max = {}
-        sums = {}
         weights = {}
+        sums = {}
 
         def multiply(i, halves=range(HALVES)):
             j, b = divmod(i, BATCH)
@@ -166,64 +162,52 @@ def tile_latentattention_pb_t_kernel(tc, query, wq, out):
                     accum_out=sums[i][:, h : h + 1],
                 )
 
-        inverse = {}
-
-        def invert(i, heads=slice(0, HEADS)):
-            if i not in inverse:
-                inverse[i] = small.tile([P, HEADS], F32, name="inverse")
-            nc.vector.reciprocal(out=inverse[i][:, heads], in_=sums[i][:, heads])
-
-        def normalise(i, engines, heads=range(HEADS)):
-            for h in heads:
-                head = weights[i][:, h * HEAD : (h + 1) * HEAD]
-                who = assign(i)[h]
-                if who not in engines:
-                    continue
-                if who == "G":
-                    nc.gpsimd.tensor_scalar(
-                        out=head, in0=head, scalar1=inverse[i][:, h : h + 1], scalar2=0.0,
-                        op0=ALU.mult, op1=ALU.add,
-                    )
-                elif who == "V":
-                    nc.vector.tensor_scalar(
-                        out=head, in0=head, scalar1=inverse[i][:, h : h + 1], scalar2=None,
-                        op0=ALU.mult,
-                    )
-                else:
-                    nc.scalar.activation(
-                        out=head, in_=head, func=ACT.Copy, scale=inverse[i][:, h : h + 1]
-                    )
-
-        def store(i, heads=slice(0, SLOTS)):
-            j, b = divmod(i, BATCH)
-            nc.sync.dma_start(out=out_view[:, j, b, heads], in_=weights[i][:, heads])
-
-        def assign(i):
+        def dividers(i):
             if i < TILES - 4:
                 return "GGGS"
-            return "GGVS" if i < TILES - 1 else "VVSV"
+            return "GGVS" if i < TILES - 2 else "GVVV"
 
+        def finish(i):
+            j, b = divmod(i, BATCH)
+            inverse = small.tile([P, HEADS], F32)
+            nc.vector.reciprocal(out=inverse[:], in_=sums[i][:])
+            for h, engine in enumerate(dividers(i)):
+                head = weights[i][:, h * HEAD : (h + 1) * HEAD]
+                factor = inverse[:, h : h + 1]
+                if engine == "G":
+                    nc.gpsimd.tensor_scalar(
+                        out=head, in0=head, scalar1=factor, scalar2=0.0, op0=ALU.mult, op1=ALU.add
+                    )
+                elif engine == "V":
+                    nc.vector.tensor_scalar(
+                        out=head, in0=head, scalar1=factor, scalar2=None, op0=ALU.mult
+                    )
+                else:
+                    nc.scalar.activation(out=head, in_=head, func=ACT.Copy, scale=factor)
+            nc.sync.dma_start(out=out_view[:, j, b, :], in_=weights[i][:])
+
+        on_vector, on_scalar = nc.vector.tensor_copy, nc.scalar.copy
         with tc.manual_schedule():
             transpose_queries(0, [0])
-            group_weights(nc.vector.tensor_copy, 0)
-            group_weights(nc.scalar.copy, HEAD)
+            group_weights(on_vector, 0)
+            group_weights(on_scalar, HEAD)
             quantise_weights(0)
-            group_queries(nc.scalar.copy, 0, slice(0, 1))
+            group_queries(on_scalar, 0, slice(0, 1))
             transpose_queries(0, [1])
             quantise_weights(1)
-            group_queries(nc.scalar.copy, 0, slice(1, 2))
+            group_queries(on_scalar, 0, slice(1, 2))
             quantise_queries(0, 0, 1)
-            group_weights(nc.scalar.copy, 2 * HEAD + W2_ON_VECTOR, HEAD - W2_ON_VECTOR)
+            group_weights(on_scalar, 2 * HEAD + ON_VECTOR, HEAD - ON_VECTOR)
             multiply(0, [0])
-            group_weights(nc.vector.tensor_copy, 2 * HEAD, W2_ON_VECTOR)
-            group_weights(nc.scalar.copy, 3 * HEAD)
+            group_weights(on_vector, 2 * HEAD, ON_VECTOR)
+            group_weights(on_scalar, 3 * HEAD)
             quantise_queries(0, 1, 1)
             multiply(1, [0])
             maxima(0, [0])
             exponentials(0, [0, 1])
             transpose_queries(1)
             quantise_weights(2)
-            group_queries(nc.scalar.copy, 1)
+            group_queries(on_scalar, 1)
             quantise_weights(3)
             multiply(0, [1])
             maxima(1, [0])
@@ -233,46 +217,23 @@ def tile_latentattention_pb_t_kernel(tc, query, wq, out):
             exponentials(0, [2, 3])
             transpose_queries(2)
             quantise_queries(1)
-            group_queries(nc.scalar.copy, 2)
+            group_queries(on_scalar, 2)
             multiply(2)
             maxima(1, [1])
             exponentials(1, [2, 3])
             multiply(3)
-            invert(0)
-            normalise(0, "G")
-            for i in range(2, TILES - 1):
+            finish(0)
+            for i in range(2, TILES):
                 j, b = divmod(i, BATCH)
                 maxima(i)
-                exponentials(i, [0, 1])
-                if b == 1 and j + 2 < ROUNDS:
-                    group_queries(nc.vector.tensor_copy, j + 2)
-                exponentials(i, [2, 3])
-                invert(i - 1)
-                if i == 2:
-                    normalise(0, "S")
-                    store(0)
-                normalise(i - 1, "GVS")
-                store(i - 1)
+                exponentials(i)
+                finish(i - 1)
                 if b == 0 and j + 1 < ROUNDS:
                     quantise_queries(j + 1)
                 if b == 0 and j + 2 < ROUNDS:
                     transpose_queries(j + 2)
+                if b == 1 and j + 2 < ROUNDS:
+                    group_queries(on_vector, j + 2)
                 if i + 2 < TILES:
                     multiply(i + 2)
-            last = TILES - 1
-            maxima(last, [0])
-            invert(last - 1)
-            normalise(last - 1, "G")
-            maxima(last, [1])
-            exponentials(last, [0, 1])
-            normalise(last - 1, "S")
-            exponentials(last, [2, 3])
-            invert(last, slice(0, 2))
-            normalise(last - 1, "V")
-            store(last - 1)
-            normalise(last, "V", [0, 1])
-            store(last, slice(0, BANK))
-            invert(last, slice(2, 4))
-            normalise(last, "S", [2, 3])
-            normalise(last, "V", [2, 3])
-            store(last, slice(BANK, SLOTS))
+            finish(TILES - 1)

from contextlib import ExitStack

import concourse.mybir as mybir
from concourse.masks import make_identity

F32 = mybir.dt.float32
BF16 = mybir.dt.bfloat16
U32 = mybir.dt.uint32
U8 = mybir.dt.uint8
FP8X4 = mybir.dt.float8_e4m3fn_x4
ALU = mybir.AluOpType
ACT = mybir.ActivationFunctionType

P = 128
PACK = 4
BATCH = 2
TOKENS = 2048
DEPTH = 512
SLOTS = 1024
HEADS = 4
HEAD = SLOTS // HEADS
BANK = 512
HALVES = SLOTS // BANK
ROUNDS = TOKENS // P
TILES = ROUNDS * BATCH
PAIRS = DEPTH // 2
ON_VECTOR = 192

FLOPS = 2 * BATCH * TOKENS * DEPTH * SLOTS


def tile_latentattention_pb_t_kernel(tc, query, wq, out):
    nc = tc.nc
    with ExitStack() as ctx:
        keep = ctx.enter_context(tc.tile_pool(name="keep", bufs=1))
        small = ctx.enter_context(tc.tile_pool(name="small", bufs=12))
        results = ctx.enter_context(tc.tile_pool(name="results", bufs=12))
        psum_t = ctx.enter_context(tc.psum_pool(name="psum_t", bufs=2))
        psum_q = ctx.enter_context(tc.psum_pool(name="psum_q", bufs=6))

        query_view = query.rearrange("b (p j) d -> p b j d", j=ROUNDS)
        out_view = out.rearrange("(p j) b h l -> p j b (h l)", j=ROUNDS)
        wq_view = wq.rearrange("(q t) c -> q t c", t=PACK)

        q_pairs = {}
        w_raw = [keep.tile([P, PACK, BANK], BF16, name="w_raw%d" % half) for half in range(HALVES)]

        def load_weights(half):
            nc.sync.dma_start(out=w_raw[half][:], in_=wq_view[:, :, half * BANK : (half + 1) * BANK])

        load_weights(0)
        for b in range(BATCH):
            row = keep.tile([P, DEPTH], BF16, name="q_first%d" % b)
            nc.sync.dma_start(out=row[:], in_=query_view[:, b, 0, :])
            q_pairs[(0, b)] = row[:].bitcast(F32)
        load_weights(1)
        for first in (1, 2, 4, 8):
            piece = keep.tile([P, BATCH, first, DEPTH], BF16, name="q_raw%d" % first)
            nc.sync.dma_start(out=piece[:], in_=query_view[:, :, first : 2 * first, :])
            for j in range(first):
                for b in range(BATCH):
                    q_pairs[(first + j, b)] = piece[:].bitcast(F32)[:, b, j, :]

        ident = keep.tile([P, P], F32)
        make_identity(nc, ident[:])
        zero = keep.tile([P, 1], F32)
        one = keep.tile([P, 1], F32)
        nc.vector.memset(zero[:], 0.0)
        nc.scalar.activation(out=one[:], in_=zero[:], func=ACT.Exp)

        q_grouped = keep.tile([P, ROUNDS, BATCH, P, PACK], BF16, align_bytes=64)
        q_codes = keep.tile([P, ROUNDS, BATCH * P], U32, align_bytes=64)
        q_scales = keep.tile([P, ROUNDS, BATCH * P], U8, align_bytes=64)
        w_grouped = keep.tile([P, SLOTS, PACK], BF16, align_bytes=64)
        w_codes = keep.tile([P, SLOTS], U32, align_bytes=64)
        w_scales = keep.tile([P, SLOTS], U8, align_bytes=64)

        turned = {}

        def transpose_queries(j, rows=range(BATCH)):
            turned[j] = psum_t.tile([P, BATCH, 2, P], F32, name="turned")
            for b in rows:
                for u in range(2):
                    nc.tensor.transpose(
                        turned[j][:, b, u, :], q_pairs[(j, b)][:, u:PAIRS:2], ident[:]
                    )

        def group_queries(copy, j, rows=slice(0, BATCH)):
            copy(
                out=q_grouped[:, j, rows].bitcast(F32),
                in_=turned[j][:, rows].rearrange("p b u r -> p b r u"),
            )

        def quantise_queries(j, first=0, count=BATCH):
            cols = slice(first * P, (first + count) * P)
            nc.vector.quantize_mx(
                out=q_codes[:, j, cols].bitcast(FP8X4),
                scales=q_scales[:, j, cols],
                in_=q_grouped[:, j, first : first + count].rearrange("p b r t -> p (b r t)"),
            )

        def group_weights(copy, first, count=HEAD):
            half, at = divmod(first, BANK)
            copy(
                out=w_grouped[:, first : first + count, :].rearrange("p (c i) t -> p c t i", i=4),
                in_=w_raw[half][:, :, at : at + count].rearrange("p t (c i) -> p c t i", i=4),
            )

        def quantise_weights(h):
            cols = slice(h * HEAD, (h + 1) * HEAD)
            nc.vector.quantize_mx(
                out=w_codes[:, cols].bitcast(FP8X4),
                scales=w_scales[:, cols],
                in_=w_grouped[:, cols, :].rearrange("p c t -> p (c t)"),
            )

        scores = {}
        neg_max = {}
        weights = {}
        sums = {}

        def multiply(i, halves=range(HALVES)):
            j, b = divmod(i, BATCH)
            for half in halves:
                cols = slice(half * BANK, (half + 1) * BANK)
                bank = psum_q.tile([P, BANK], F32, name="bank")
                nc.tensor.matmul_mx(
                    out=bank[:],
                    lhsT=q_codes[:, j, b * P : (b + 1) * P].bitcast(FP8X4),
                    lhsT_scale=q_scales[:, j, b * P : (b + 1) * P],
                    rhs=w_codes[:, cols].bitcast(FP8X4),
                    rhs_scale=w_scales[:, cols],
                    start=True,
                    stop=True,
                )
                scores[(i, half)] = bank

        def maxima(i, halves=range(HALVES)):
            if i not in neg_max:
                neg_max[i] = small.tile([P, HEADS], F32, name="neg_max")
            for half in halves:
                nc.vector.tensor_reduce(
                    out=neg_max[i][:, 2 * half : 2 * half + 2],
                    in_=scores[(i, half)][:].rearrange("p (h l) -> p h l", l=HEAD),
                    axis=mybir.AxisListType.X,
                    op=ALU.max,
                    negate=True,
                )

        def exponentials(i, heads=range(HEADS)):
            if i not in weights:
                weights[i] = results.tile([P, SLOTS], F32, name="weights")
                sums[i] = small.tile([P, HEADS], F32, name="sums")
            for h in heads:
                half, side = divmod(h, 2)
                nc.scalar.activation(
                    out=weights[i][:, h * HEAD : (h + 1) * HEAD],
                    in_=scores[(i, half)][:, side * HEAD : (side + 1) * HEAD],
                    func=ACT.Exp,
                    bias=neg_max[i][:, h : h + 1],
                    scale=1.0,
                    accum_out=sums[i][:, h : h + 1],
                )

        def dividers(i):
            if i < TILES - 4:
                return "GGGS"
            return "GGVS" if i < TILES - 2 else "GVVV"

        def finish(i):
            j, b = divmod(i, BATCH)
            inverse = small.tile([P, HEADS], F32)
            nc.vector.reciprocal(out=inverse[:], in_=sums[i][:])
            for h, engine in enumerate(dividers(i)):
                head = weights[i][:, h * HEAD : (h + 1) * HEAD]
                factor = inverse[:, h : h + 1]
                if engine == "G":
                    nc.gpsimd.tensor_scalar(
                        out=head, in0=head, scalar1=factor, scalar2=0.0, op0=ALU.mult, op1=ALU.add
                    )
                elif engine == "V":
                    nc.vector.tensor_scalar(
                        out=head, in0=head, scalar1=factor, scalar2=None, op0=ALU.mult
                    )
                else:
                    nc.scalar.activation(out=head, in_=head, func=ACT.Copy, scale=factor)
            nc.sync.dma_start(out=out_view[:, j, b, :], in_=weights[i][:])

        on_vector, on_scalar = nc.vector.tensor_copy, nc.scalar.copy
        with tc.manual_schedule():
            transpose_queries(0, [0])
            group_weights(on_vector, 0)
            group_weights(on_scalar, HEAD)
            quantise_weights(0)
            group_queries(on_scalar, 0, slice(0, 1))
            transpose_queries(0, [1])
            quantise_weights(1)
            group_queries(on_scalar, 0, slice(1, 2))
            quantise_queries(0, 0, 1)
            group_weights(on_scalar, 2 * HEAD + ON_VECTOR, HEAD - ON_VECTOR)
            multiply(0, [0])
            group_weights(on_vector, 2 * HEAD, ON_VECTOR)
            group_weights(on_scalar, 3 * HEAD)
            quantise_queries(0, 1, 1)
            multiply(1, [0])
            maxima(0, [0])
            exponentials(0, [0, 1])
            transpose_queries(1)
            quantise_weights(2)
            group_queries(on_scalar, 1)
            quantise_weights(3)
            multiply(0, [1])
            maxima(1, [0])
            exponentials(1, [0, 1])
            multiply(1, [1])
            maxima(0, [1])
            exponentials(0, [2, 3])
            transpose_queries(2)
            quantise_queries(1)
            group_queries(on_scalar, 2)
            multiply(2)
            maxima(1, [1])
            exponentials(1, [2, 3])
            multiply(3)
            finish(0)
            for i in range(2, TILES):
                j, b = divmod(i, BATCH)
                maxima(i)
                exponentials(i)
                finish(i - 1)
                if b == 0 and j + 1 < ROUNDS:
                    quantise_queries(j + 1)
                if b == 0 and j + 2 < ROUNDS:
                    transpose_queries(j + 2)
                if b == 1 and j + 2 < ROUNDS:
                    group_queries(on_vector, j + 2)
                if i + 2 < TILES:
                    multiply(i + 2)
            finish(TILES - 1)
